import numpy as np
import ml_dtypes

BF16 = ml_dtypes.bfloat16


def bf(x):
    return np.asarray(x, np.float32).astype(BF16)


def f32(x):
    return np.asarray(x, np.float32)


def f64(x):
    return np.asarray(x).astype(np.float64)


def striped(idx):
    return np.tile(idx.reshape(-1, 16).T, (8, 1))


C, D, S, H, K, N = 128, 128, 2048, 1024, 8, 8192
TAU = 1.0 / np.sqrt(C)


def setup_inputs():
    x = f32(np.random.standard_normal((C, S)))
    zd = bf(np.random.standard_normal((D, H)))
    wq = bf(2.0 * np.random.standard_normal((D, C)) / np.sqrt(D))
    bq = f32(0.1 * np.random.standard_normal((C, 1)))
    idx = np.concatenate([np.random.permutation(S)[:H] for _ in range(K)])
    return {"x": x, "zd": zd, "wq": wq, "bq": bq, "offs": striped(idx)}


def reference(x, zd, wq, bq, offs):
    idx = offs[:16].T.reshape(-1)
    q = f64(wq).T @ f64(zd) + f64(bq)
    return f64(x)[:, idx] * np.tile(q, (1, K)) * TAU

@@ -1,0 +1,51 @@
+import math
+
+import concourse.mybir as mybir
+
+F32, BF16, U16 = mybir.dt.float32, mybir.dt.bfloat16, mybir.dt.uint16
+MULT = mybir.AluOpType.mult
+IDENTITY = mybir.ActivationFunctionType.Identity
+
+P = 128
+SOURCES = 2048
+DESTS = 1024
+SLOTS = 8
+BANK = 512
+TAU = 1.0 / math.sqrt(P)
+
+FLOPS = 2 * P * P * DESTS
+
+
+def tile_bayesgatlayer_kernel(tc, x, zd, wq, bq, offs, out):
+    nc = tc.nc
+    with (
+        tc.tile_pool(name="held", bufs=1) as held,
+        tc.tile_pool(name="products", bufs=4) as products,
+        tc.psum_pool(name="psum", bufs=2) as psum,
+    ):
+        offsets = held.tile([P, SLOTS * DESTS // 16], U16, name="offsets")
+        nc.sync.dma_start(offsets[:], offs)
+        keys = held.tile([P, SOURCES], F32, name="keys")
+        nc.sync.dma_start(keys[:], x)
+        weights = held.tile([P, P], BF16, name="weights")
+        nc.scalar.dma_start(weights[:], wq)
+        dests = held.tile([P, DESTS], BF16, name="dests")
+        nc.scalar.dma_start(dests[:], zd)
+        bias = held.tile([P, 1], F32, name="bias")
+        nc.scalar.dma_start(bias[:], bq)
+
+        bias_tau = held.tile([P, 1], F32, name="bias_tau")
+        nc.scalar.mul(bias_tau[:], bias[:], TAU)
+        query = held.tile([P, DESTS], F32, name="query")
+        for b in range(DESTS // BANK):
+            cols = slice(b * BANK, (b + 1) * BANK)
+            projected = psum.tile([P, BANK], F32, name="projected")
+            nc.tensor.matmul(projected[:], weights[:], dests[:, cols], start=True, stop=True)
+            nc.scalar.activation(query[:, cols], projected[:], IDENTITY, bias=bias_tau[:], scale=TAU)
+
+        for k in range(SLOTS):
+            slot_offsets = offsets[:, k * (DESTS // 16) : (k + 1) * (DESTS // 16)]
+            product = products.tile([P, DESTS], F32, name="product")
+            nc.vector.tensor_tensor(product[:], keys[:].indirect(slot_offsets), query[:], MULT)
+            store_queue = nc.sync if k % 2 == 0 else nc.scalar
+            store_queue.dma_start(out[:, k * DESTS : (k + 1) * DESTS], product[:])

@@ -3,8 +3,7 @@ import math
 import concourse.mybir as mybir
 
 F32, BF16, U16 = mybir.dt.float32, mybir.dt.bfloat16, mybir.dt.uint16
-MULT = mybir.AluOpType.mult
-IDENTITY = mybir.ActivationFunctionType.Identity
+ADD, MULT = mybir.AluOpType.add, mybir.AluOpType.mult
 
 P = 128
 SOURCES = 2048
@@ -23,29 +22,33 @@ def tile_bayesgatlayer_kernel(tc, x, zd, wq, bq, offs, out):
         tc.tile_pool(name="products", bufs=4) as products,
         tc.psum_pool(name="psum", bufs=2) as psum,
     ):
+        weights = held.tile([P, P], BF16, name="weights")
+        nc.sync.dma_start(weights[:], wq)
+        dests = held.tile([P, DESTS], BF16, name="dests")
+        nc.sync.dma_start(dests[:], zd)
         offsets = held.tile([P, SLOTS * DESTS // 16], U16, name="offsets")
         nc.sync.dma_start(offsets[:], offs)
-        keys = held.tile([P, SOURCES], F32, name="keys")
-        nc.sync.dma_start(keys[:], x)
-        weights = held.tile([P, P], BF16, name="weights")
-        nc.scalar.dma_start(weights[:], wq)
-        dests = held.tile([P, DESTS], BF16, name="dests")
-        nc.scalar.dma_start(dests[:], zd)
         bias = held.tile([P, 1], F32, name="bias")
         nc.scalar.dma_start(bias[:], bq)
+        keys = held.tile([P, SOURCES], F32, name="keys")
+        nc.scalar.dma_start(keys[:], x)
 
-        bias_tau = held.tile([P, 1], F32, name="bias_tau")
-        nc.scalar.mul(bias_tau[:], bias[:], TAU)
         query = held.tile([P, DESTS], F32, name="query")
         for b in range(DESTS // BANK):
             cols = slice(b * BANK, (b + 1) * BANK)
             projected = psum.tile([P, BANK], F32, name="projected")
             nc.tensor.matmul(projected[:], weights[:], dests[:, cols], start=True, stop=True)
-            nc.scalar.activation(query[:, cols], projected[:], IDENTITY, bias=bias_tau[:], scale=TAU)
+            nc.vector.tensor_scalar(query[:, cols], projected[:], bias[:], TAU, ADD, MULT)
 
-        for k in range(SLOTS):
-            slot_offsets = offsets[:, k * (DESTS // 16) : (k + 1) * (DESTS // 16)]
-            product = products.tile([P, DESTS], F32, name="product")
-            nc.vector.tensor_tensor(product[:], keys[:].indirect(slot_offsets), query[:], MULT)
-            store_queue = nc.sync if k % 2 == 0 else nc.scalar
-            store_queue.dma_start(out[:, k * DESTS : (k + 1) * DESTS], product[:])
+        widths = [DESTS] * (SLOTS - 1) + [DESTS // 2, DESTS // 4, DESTS // 4]
+        first = 0
+        for i, width in enumerate(widths):
+            piece_offsets = offsets[:, first // 16 : (first + width) // 16]
+            dest = first % DESTS
+            product = products.tile([P, width], F32, name="product")
+            nc.vector.tensor_tensor(
+                product[:], keys[:].indirect(piece_offsets), query[:, dest : dest + width], MULT
+            )
+            store_queue = nc.sync if i % 2 == 0 else nc.scalar
+            store_queue.dma_start(out[:, first : first + width], product[:])
+            first += width

@@ -40,15 +40,9 @@ def tile_bayesgatlayer_kernel(tc, x, zd, wq, bq, offs, out):
             nc.tensor.matmul(projected[:], weights[:], dests[:, cols], start=True, stop=True)
             nc.vector.tensor_scalar(query[:, cols], projected[:], bias[:], TAU, ADD, MULT)
 
-        widths = [DESTS] * (SLOTS - 1) + [DESTS // 2, DESTS // 4, DESTS // 4]
-        first = 0
-        for i, width in enumerate(widths):
-            piece_offsets = offsets[:, first // 16 : (first + width) // 16]
-            dest = first % DESTS
-            product = products.tile([P, width], F32, name="product")
-            nc.vector.tensor_tensor(
-                product[:], keys[:].indirect(piece_offsets), query[:, dest : dest + width], MULT
-            )
-            store_queue = nc.sync if i % 2 == 0 else nc.scalar
-            store_queue.dma_start(out[:, first : first + width], product[:])
-            first += width
+        for k in range(SLOTS):
+            slot_offsets = offsets[:, k * (DESTS // 16) : (k + 1) * (DESTS // 16)]
+            product = products.tile([P, DESTS], F32, name="product")
+            nc.vector.tensor_tensor(product[:], keys[:].indirect(slot_offsets), query[:], MULT)
+            store_queue = nc.sync if k % 2 == 0 else nc.scalar
+            store_queue.dma_start(out[:, k * DESTS : (k + 1) * DESTS], product[:])

@@ -23,15 +23,15 @@ def tile_bayesgatlayer_kernel(tc, x, zd, wq, bq, offs, out):
         tc.psum_pool(name="psum", bufs=2) as psum,
     ):
         weights = held.tile([P, P], BF16, name="weights")
-        nc.sync.dma_start(weights[:], wq)
+        nc.scalar.dma_start(weights[:], wq)
         dests = held.tile([P, DESTS], BF16, name="dests")
-        nc.sync.dma_start(dests[:], zd)
-        offsets = held.tile([P, SLOTS * DESTS // 16], U16, name="offsets")
-        nc.sync.dma_start(offsets[:], offs)
-        bias = held.tile([P, 1], F32, name="bias")
-        nc.scalar.dma_start(bias[:], bq)
+        nc.scalar.dma_start(dests[:], zd)
         keys = held.tile([P, SOURCES], F32, name="keys")
         nc.scalar.dma_start(keys[:], x)
+        bias = held.tile([P, 1], F32, name="bias")
+        nc.sync.dma_start(bias[:], bq)
+        offsets = held.tile([P, SLOTS * DESTS // 16], U16, name="offsets")
+        nc.sync.dma_start(offsets[:], offs)
 
         query = held.tile([P, DESTS], F32, name="query")
         for b in range(DESTS // BANK):
@@ -40,9 +40,15 @@ def tile_bayesgatlayer_kernel(tc, x, zd, wq, bq, offs, out):
             nc.tensor.matmul(projected[:], weights[:], dests[:, cols], start=True, stop=True)
             nc.vector.tensor_scalar(query[:, cols], projected[:], bias[:], TAU, ADD, MULT)
 
-        for k in range(SLOTS):
-            slot_offsets = offsets[:, k * (DESTS // 16) : (k + 1) * (DESTS // 16)]
-            product = products.tile([P, DESTS], F32, name="product")
-            nc.vector.tensor_tensor(product[:], keys[:].indirect(slot_offsets), query[:], MULT)
-            store_queue = nc.sync if k % 2 == 0 else nc.scalar
-            store_queue.dma_start(out[:, k * DESTS : (k + 1) * DESTS], product[:])
+        widths = [DESTS] * (SLOTS - 1) + [DESTS // 2, DESTS // 4, DESTS // 4]
+        first = 0
+        for i, width in enumerate(widths):
+            piece_offsets = offsets[:, first // 16 : (first + width) // 16]
+            dest = first % DESTS
+            product = products.tile([P, width], F32, name="product")
+            nc.vector.tensor_tensor(
+                product[:], keys[:].indirect(piece_offsets), query[:, dest : dest + width], MULT
+            )
+            store_queue = nc.sync if i % 2 == 0 else nc.scalar
+            store_queue.dma_start(out[:, first : first + width], product[:])
+            first += width

@@ -26,12 +26,13 @@ def tile_bayesgatlayer_kernel(tc, x, zd, wq, bq, offs, out):
         nc.scalar.dma_start(weights[:], wq)
         dests = held.tile([P, DESTS], BF16, name="dests")
         nc.scalar.dma_start(dests[:], zd)
-        keys = held.tile([P, SOURCES], F32, name="keys")
-        nc.scalar.dma_start(keys[:], x)
         bias = held.tile([P, 1], F32, name="bias")
         nc.sync.dma_start(bias[:], bq)
         offsets = held.tile([P, SLOTS * DESTS // 16], U16, name="offsets")
         nc.sync.dma_start(offsets[:], offs)
+        keys = held.tile([P, SOURCES], F32, name="keys")
+        nc.scalar.dma_start(keys[:, : SOURCES // 2], x[:, : SOURCES // 2])
+        nc.sync.dma_start(keys[:, SOURCES // 2 :], x[:, SOURCES // 2 :])
 
         query = held.tile([P, DESTS], F32, name="query")
         for b in range(DESTS // BANK):

@@ -25,9 +25,9 @@ def tile_bayesgatlayer_kernel(tc, x, zd, wq, bq, offs, out):
         weights = held.tile([P, P], BF16, name="weights")
         nc.scalar.dma_start(weights[:], wq)
         dests = held.tile([P, DESTS], BF16, name="dests")
-        nc.scalar.dma_start(dests[:], zd)
+        nc.sync.dma_start(dests[:], zd)
         bias = held.tile([P, 1], F32, name="bias")
-        nc.sync.dma_start(bias[:], bq)
+        nc.scalar.dma_start(bias[:], bq)
         offsets = held.tile([P, SLOTS * DESTS // 16], U16, name="offsets")
         nc.sync.dma_start(offsets[:], offs)
         keys = held.tile([P, SOURCES], F32, name="keys")

@@ -34,22 +34,27 @@ def tile_bayesgatlayer_kernel(tc, x, zd, wq, bq, offs, out):
         nc.scalar.dma_start(keys[:, : SOURCES // 2], x[:, : SOURCES // 2])
         nc.sync.dma_start(keys[:, SOURCES // 2 :], x[:, SOURCES // 2 :])
 
-        query = held.tile([P, DESTS], F32, name="query")
+        query = held.tile([P, 2 * DESTS], F32, name="query")
         for b in range(DESTS // BANK):
             cols = slice(b * BANK, (b + 1) * BANK)
             projected = psum.tile([P, BANK], F32, name="projected")
             nc.tensor.matmul(projected[:], weights[:], dests[:, cols], start=True, stop=True)
             nc.vector.tensor_scalar(query[:, cols], projected[:], bias[:], TAU, ADD, MULT)
+        nc.scalar.copy(query[:, DESTS:], query[:, :DESTS])
 
-        widths = [DESTS] * (SLOTS - 1) + [DESTS // 2, DESTS // 4, DESTS // 4]
+        widths = [DESTS, 2 * DESTS, 2 * DESTS, DESTS, DESTS, DESTS // 2, DESTS // 4, DESTS // 4]
         first = 0
-        for i, width in enumerate(widths):
+        stores = 0
+        for width in widths:
             piece_offsets = offsets[:, first // 16 : (first + width) // 16]
             dest = first % DESTS
             product = products.tile([P, width], F32, name="product")
             nc.vector.tensor_tensor(
                 product[:], keys[:].indirect(piece_offsets), query[:, dest : dest + width], MULT
             )
-            store_queue = nc.sync if i % 2 == 0 else nc.scalar
-            store_queue.dma_start(out[:, first : first + width], product[:])
+            for begin in range(0, width, DESTS):
+                end = min(begin + DESTS, width)
+                store_queue = nc.sync if stores % 2 == 0 else nc.scalar
+                store_queue.dma_start(out[:, first + begin : first + end], product[:, begin:end])
+                stores += 1
             first += width

@@ -12,6 +12,10 @@ SLOTS = 8
 BANK = 512
 TAU = 1.0 / math.sqrt(P)
 
+BEFORE_KEYS_ON_SCALAR = 2 * P
+BEFORE_KEYS_ON_SYNC = 2 * DESTS + 2 * SLOTS * DESTS // 16
+KEYS_BY_SCALAR = (4 * SOURCES + BEFORE_KEYS_ON_SYNC - BEFORE_KEYS_ON_SCALAR) // 2 // 4
+
 FLOPS = 2 * P * P * DESTS
 
 
@@ -31,8 +35,8 @@ def tile_bayesgatlayer_kernel(tc, x, zd, wq, bq, offs, out):
         offsets = held.tile([P, SLOTS * DESTS // 16], U16, name="offsets")
         nc.sync.dma_start(offsets[:], offs)
         keys = held.tile([P, SOURCES], F32, name="keys")
-        nc.scalar.dma_start(keys[:, : SOURCES // 2], x[:, : SOURCES // 2])
-        nc.sync.dma_start(keys[:, SOURCES // 2 :], x[:, SOURCES // 2 :])
+        nc.scalar.dma_start(keys[:, :KEYS_BY_SCALAR], x[:, :KEYS_BY_SCALAR])
+        nc.sync.dma_start(keys[:, KEYS_BY_SCALAR:], x[:, KEYS_BY_SCALAR:])
 
         query = held.tile([P, 2 * DESTS], F32, name="query")
         for b in range(DESTS // BANK):

@@ -44,21 +44,28 @@ def tile_bayesgatlayer_kernel(tc, x, zd, wq, bq, offs, out):
             projected = psum.tile([P, BANK], F32, name="projected")
             nc.tensor.matmul(projected[:], weights[:], dests[:, cols], start=True, stop=True)
             nc.vector.tensor_scalar(query[:, cols], projected[:], bias[:], TAU, ADD, MULT)
-        nc.scalar.copy(query[:, DESTS:], query[:, :DESTS])
+            nc.scalar.copy(query[:, DESTS + cols.start : DESTS + cols.stop], query[:, cols])
 
-        widths = [DESTS, 2 * DESTS, 2 * DESTS, DESTS, DESTS, DESTS // 2, DESTS // 4, DESTS // 4]
-        first = 0
+        last_slot = (SLOTS - 1) * DESTS
+        runs = [
+            (last_slot, DESTS // 4),
+            (0, 2 * DESTS),
+            (2 * DESTS, 2 * DESTS),
+            (4 * DESTS, 2 * DESTS),
+            (6 * DESTS, DESTS),
+            (last_slot + DESTS // 4, DESTS // 2),
+            (last_slot + 3 * DESTS // 4, DESTS // 4),
+        ]
         stores = 0
-        for width in widths:
-            piece_offsets = offsets[:, first // 16 : (first + width) // 16]
+        for first, width in runs:
+            run_offsets = offsets[:, first // 16 : (first + width) // 16]
             dest = first % DESTS
             product = products.tile([P, width], F32, name="product")
             nc.vector.tensor_tensor(
-                product[:], keys[:].indirect(piece_offsets), query[:, dest : dest + width], MULT
+                product[:], keys[:].indirect(run_offsets), query[:, dest : dest + width], MULT
             )
             for begin in range(0, width, DESTS):
                 end = min(begin + DESTS, width)
                 store_queue = nc.sync if stores % 2 == 0 else nc.scalar
                 store_queue.dma_start(out[:, first + begin : first + end], product[:, begin:end])
                 stores += 1
-            first += width

import math

import concourse.mybir as mybir

F32, BF16, U16 = mybir.dt.float32, mybir.dt.bfloat16, mybir.dt.uint16
ADD, MULT = mybir.AluOpType.add, mybir.AluOpType.mult

P = 128
SOURCES = 2048
DESTS = 1024
SLOTS = 8
BANK = 512
TAU = 1.0 / math.sqrt(P)

BEFORE_KEYS_ON_SCALAR = 2 * P
BEFORE_KEYS_ON_SYNC = 2 * DESTS + 2 * SLOTS * DESTS // 16
KEYS_BY_SCALAR = (4 * SOURCES + BEFORE_KEYS_ON_SYNC - BEFORE_KEYS_ON_SCALAR) // 2 // 4

FLOPS = 2 * P * P * DESTS


def tile_bayesgatlayer_kernel(tc, x, zd, wq, bq, offs, out):
    nc = tc.nc
    with (
        tc.tile_pool(name="held", bufs=1) as held,
        tc.tile_pool(name="products", bufs=4) as products,
        tc.psum_pool(name="psum", bufs=2) as psum,
    ):
        weights = held.tile([P, P], BF16, name="weights")
        nc.scalar.dma_start(weights[:], wq)
        dests = held.tile([P, DESTS], BF16, name="dests")
        nc.sync.dma_start(dests[:], zd)
        bias = held.tile([P, 1], F32, name="bias")
        nc.scalar.dma_start(bias[:], bq)
        offsets = held.tile([P, SLOTS * DESTS // 16], U16, name="offsets")
        nc.sync.dma_start(offsets[:], offs)
        keys = held.tile([P, SOURCES], F32, name="keys")
        nc.scalar.dma_start(keys[:, :KEYS_BY_SCALAR], x[:, :KEYS_BY_SCALAR])
        nc.sync.dma_start(keys[:, KEYS_BY_SCALAR:], x[:, KEYS_BY_SCALAR:])

        query = held.tile([P, 2 * DESTS], F32, name="query")
        for b in range(DESTS // BANK):
            cols = slice(b * BANK, (b + 1) * BANK)
            projected = psum.tile([P, BANK], F32, name="projected")
            nc.tensor.matmul(projected[:], weights[:], dests[:, cols], start=True, stop=True)
            nc.vector.tensor_scalar(query[:, cols], projected[:], bias[:], TAU, ADD, MULT)
            nc.scalar.copy(query[:, DESTS + cols.start : DESTS + cols.stop], query[:, cols])

        last_slot = (SLOTS - 1) * DESTS
        runs = [
            (last_slot, DESTS // 4),
            (0, 2 * DESTS),
            (2 * DESTS, 2 * DESTS),
            (4 * DESTS, 2 * DESTS),
            (6 * DESTS, DESTS),
            (last_slot + DESTS // 4, DESTS // 2),
            (last_slot + 3 * DESTS // 4, DESTS // 4),
        ]
        stores = 0
        for first, width in runs:
            run_offsets = offsets[:, first // 16 : (first + width) // 16]
            dest = first % DESTS
            product = products.tile([P, width], F32, name="product")
            nc.vector.tensor_tensor(
                product[:], keys[:].indirect(run_offsets), query[:, dest : dest + width], MULT
            )
            for begin in range(0, width, DESTS):
                end = min(begin + DESTS, width)
                store_queue = nc.sync if stores % 2 == 0 else nc.scalar
                store_queue.dma_start(out[:, first + begin : first + end], product[:, begin:end])
                stores += 1
